import numpy as np
import ml_dtypes


def mxq(x, axis, fmt="e4m3"):
    dtype, down = {"e4m3": (ml_dtypes.float8_e4m3fn, 7), "e5m2": (ml_dtypes.float8_e5m2, 14)}[fmt]
    v = np.moveaxis(np.asarray(x, np.float32).astype(ml_dtypes.bfloat16).astype(np.float64), axis, -1)
    blocks = v.reshape(v.shape[:-1] + (-1, 32))
    amax = np.abs(blocks).max(-1, keepdims=True)
    byte = np.maximum(np.where(amax > 0, np.frexp(amax)[1] - 1 + 127, 0) - down, 1)
    scale = np.exp2(byte - 127.0)
    codes = (blocks / scale).astype(np.float32).astype(dtype).astype(np.float64)
    return np.moveaxis((codes * scale).reshape(v.shape), -1, axis)


WIDE = False


def mx_kscale(k):
    if not WIDE:
        return np.ones(k)
    levels = np.array([10, -10, 5, -5, 0])
    a = np.random.permutation(np.resize(levels, k // 512 * 4)).reshape(k // 512, 4)
    idx = np.arange(k)
    return np.exp2(a[idx // 512, idx % 128 // 32])


BF16 = ml_dtypes.bfloat16


def bf(x):
    return np.asarray(x, np.float32).astype(BF16)


def f64(x):
    return np.asarray(x).astype(np.float64)


B, N, F, K = 16, 512, 512, 256
BN_EPS = 1e-5
NORM_EPS = 1e-12


def setup_inputs():
    s, t = mx_kscale(N), mx_kscale(F)
    deg = np.random.uniform(0.5, 1.5, size=(B, N, 1))
    return {"x": bf(np.random.standard_normal((B, N, F)) * 0.5 / s[:, None] * t),
            "adj": bf(np.random.uniform(size=(B, N, N)) * deg * 4.0 / np.sqrt(N) * s),
            "W": bf(np.random.standard_normal((F, K)) / np.sqrt(F) / t[:, None]),
            "b": bf(np.random.standard_normal(K) * 0.2)}


def reference(x, adj, W, b):
    agg = mxq(f64(adj), 2, "e4m3") @ mxq(f64(x), 1, "e4m3")
    h = (mxq(agg, 2, "e4m3") @ mxq(f64(W), 0, "e4m3")) + f64(b)
    nrm = np.sqrt(np.sum(h * h, axis=2, keepdims=True))
    h = h / np.maximum(nrm, NORM_EPS)
    h = np.maximum(h, 0.0)
    mean = np.mean(h, axis=(0, 2), keepdims=True)
    var = np.var(h, axis=(0, 2), keepdims=True)
    return (h - mean) / np.sqrt(var + BN_EPS)

@@ -1,0 +1,344 @@
+from contextlib import ExitStack
+
+import concourse.mybir as mybir
+from concourse.masks import make_identity
+
+F32 = mybir.dt.float32
+BF16 = mybir.dt.bfloat16
+U32 = mybir.dt.uint32
+U8 = mybir.dt.uint8
+FP8X4 = mybir.dt.float8_e4m3fn_x4
+ALU = mybir.AluOpType
+ACT = mybir.ActivationFunctionType
+
+P = 128
+PACK = 4
+GRAPHS, NODES, FEATS, OUTS = 16, 512, 512, 256
+NODE_TILES = NODES // P
+FEAT_TILES = FEATS // P
+PAIR = 2
+GROUPS = GRAPHS // PAIR
+UNITS = NODE_TILES * GROUPS
+BN_FIELDS = 6
+BN_EPS = 1e-5
+NORM_EPS = 1e-12
+
+FLOPS = 2 * GRAPHS * NODES * NODES * FEATS + 2 * GRAPHS * NODES * FEATS * OUTS
+
+LAG_LOAD = 0
+LAG_X_REGROUP = 2
+LAG_X_QUANT = 3
+LAG_TRANSPOSE = 3
+LAG_ADJ_OUT = 4
+LAG_ADJ_QUANT = 5
+LAG_AGG = 6
+LAG_AGG_OUT = 7
+LAG_AGG_QUANT = 8
+LAG_H = 9
+LAG_BIAS = 10
+LAG_RELU = 11
+LAG_BN = 12
+LAG_NORMS = 13
+LAG_MOMENTS = 14
+LAG_FACTORS = 15
+LAG_APPLY = LAG_FACTORS + GROUPS
+LAG_STORE = LAG_APPLY + 1
+
+
+def tile_routingassignment_pa_t_kernel(tc, x, adj, W, b, out):
+    nc = tc.nc
+    with ExitStack() as ctx:
+        ctx.enter_context(tc.manual_schedule())
+
+        def pool(name, bufs):
+            return ctx.enter_context(tc.tile_pool(name=name, bufs=bufs))
+
+        keep = pool("keep", 1)
+        x_raw_pool = pool("x_raw", PAIR * (LAG_X_REGROUP - LAG_LOAD + 1))
+        x_grouped_pool = pool("x_grouped", PAIR * (LAG_X_QUANT - LAG_X_REGROUP + 1))
+        adj_raw_pool = pool("adj_raw", LAG_TRANSPOSE - LAG_LOAD + 1)
+        hand_over = pool("hand_over", 2)
+        result_pool = pool("result", LAG_STORE - LAG_RELU + 1)
+        unread_pool = pool("unread", 4)
+        per_node_tile = pool("per_node_tile", 2)
+        psum_words = ctx.enter_context(tc.psum_pool(name="psum_words", bufs=2))
+        psum_agg = ctx.enter_context(tc.psum_pool(name="psum_agg", bufs=2 * PAIR))
+        psum_h = ctx.enter_context(tc.psum_pool(name="psum_h", bufs=2))
+
+        x_rows = x.rearrange("g (u q e) f -> g q u (e f)", u=2, e=2)
+        adj_rows = adj.rearrange("g (p t) m -> p g t m", t=NODE_TILES)
+        out_rows = out.rearrange("g (p t) k -> p g t k", t=NODE_TILES)
+
+        w_raw = keep.tile([P, FEAT_TILES, OUTS], BF16)
+        nc.scalar.dma_start(out=w_raw[:], in_=W.rearrange("(t c) k -> c t k", t=FEAT_TILES))
+        bias_row = keep.tile([P, OUTS], BF16)
+        nc.gpsimd.memset(bias_row[:], 0.0)
+        nc.scalar.dma_start(out=bias_row[0:1, :], in_=b.rearrange("(o k) -> o k", o=1))
+        ones = keep.tile([P, P], BF16)
+        nc.gpsimd.memset(ones[:], 1.0)
+        identity = keep.tile([P, P], F32)
+        make_identity(nc, identity[:])
+
+        one = keep.tile([P, 1], F32)
+        nc.gpsimd.memset(one[:], 1.0)
+        nc.scalar.sqrt(out=one[:], in_=one[:])
+
+        w_grouped = keep.tile([P, OUTS, PACK], BF16, align_bytes=64)
+        nc.vector.tensor_copy(out=w_grouped[:], in_=w_raw[:].rearrange("c t k -> c k t"))
+        w_codes = keep.tile([P, OUTS], U32, align_bytes=64)
+        w_scales = keep.tile([P, OUTS], U8, align_bytes=64)
+        nc.vector.quantize_mx(
+            out=w_codes[:].bitcast(FP8X4), scales=w_scales[:], in_=w_grouped[:].rearrange("c k t -> c (k t)")
+        )
+
+        bias_bank = psum_h.tile([P, PAIR, OUTS], F32, name="h_bank")
+        nc.tensor.matmul(out=bias_bank[:, 0, :], lhsT=ones[:], rhs=bias_row[:], start=True, stop=True)
+        bias = keep.tile([P, PAIR, OUTS], F32)
+        for gi in range(PAIR):
+            nc.vector.tensor_copy(out=bias[:, gi, :], in_=bias_bank[:, 0, :])
+
+        x_codes = [keep.tile([P, FEATS], U32, align_bytes=64, name="x_codes%d" % g) for g in range(GRAPHS)]
+        x_scales = [keep.tile([P, FEATS], U8, align_bytes=64, name="x_scales%d" % g) for g in range(GRAPHS)]
+
+        x_raw, x_grouped = {}, {}
+        adj_raw, word_bank, adj_grouped, adj_codes, adj_scales = {}, {}, {}, {}, {}
+        agg_bank, agg_grouped, agg_codes, agg_scales = {}, {}, {}, {}
+        h_bank, h_sb, result = {}, {}, {}
+        square_sum, relu_stats, norm, inverse_norm, mean_var, deviation, factor, shift = {}, {}, {}, {}, {}, {}, {}, {}
+
+        def graphs_of(unit):
+            first = (unit % GROUPS) * PAIR
+            return range(first, first + PAIR)
+
+        def load(unit):
+            node_tile = unit // GROUPS
+            graphs = graphs_of(unit)
+            if node_tile == 0:
+                for g in graphs:
+                    x_raw[g] = x_raw_pool.tile([P, 2, 2 * FEATS], BF16, name="x_raw")
+                    nc.sync.dma_start(out=x_raw[g][:], in_=x_rows[g])
+            adj_raw[unit] = adj_raw_pool.tile([P, PAIR * NODES], BF16, name="adj_raw")
+            nc.sync.dma_start(
+                out=adj_raw[unit][:].rearrange("p (g m) -> p g m", g=PAIR),
+                in_=adj_rows[:, graphs[0] : graphs[0] + PAIR, node_tile, :],
+            )
+
+        def regroup_x(unit):
+            if unit >= GROUPS:
+                return
+            half = FEATS // 2
+            for g in graphs_of(unit):
+                x_grouped[g] = x_grouped_pool.tile([P, FEATS, PACK], BF16, align_bytes=64, name="x_grouped")
+                rows = x_raw[g][:].rearrange("q u (e f) -> q (u e) f", e=2)
+                nc.vector.tensor_copy(
+                    out=x_grouped[g][:, 0:half, :].rearrange("q (c i) j -> q c j i", i=4),
+                    in_=rows[:, :, 0:half].rearrange("q j (c i) -> q c j i", i=4),
+                )
+                nc.scalar.copy(
+                    out=x_grouped[g][:, half:FEATS, :].rearrange("q (c i) j -> q c j i", i=4),
+                    in_=rows[:, :, half:FEATS].rearrange("q j (c i) -> q c j i", i=4),
+                )
+
+        def quantise_x(unit):
+            if unit >= GROUPS:
+                return
+            for g in graphs_of(unit):
+                nc.vector.quantize_mx(
+                    out=x_codes[g][:].bitcast(FP8X4),
+                    scales=x_scales[g][:],
+                    in_=x_grouped[g][:].rearrange("q f j -> q (f j)"),
+                )
+
+        def transpose_adj(unit):
+            word_bank[unit] = psum_words.tile([P, PAIR, 2, P], F32, name="word_bank")
+            words = adj_raw[unit][:].bitcast(F32)
+            for gi in range(PAIR):
+                for u in range(2):
+                    first = (gi * 2 + u) * P
+                    nc.tensor.transpose(
+                        out=word_bank[unit][:, gi, u, :], in_=words[:, first : first + P], identity=identity[:]
+                    )
+
+        def copy_adj_out(unit):
+            adj_grouped[unit] = hand_over.tile([P, PAIR * P * PACK], BF16, align_bytes=64, name="adj_grouped")
+            nc.scalar.copy(
+                out=adj_grouped[unit][:].bitcast(F32).rearrange("q (g n u) -> q g n u", g=PAIR, u=2),
+                in_=word_bank[unit][:].rearrange("q g u n -> q g n u"),
+            )
+
+        def quantise_adj(unit):
+            adj_codes[unit] = hand_over.tile([P, PAIR * P], U32, align_bytes=64, name="adj_codes")
+            adj_scales[unit] = hand_over.tile([P, PAIR * P], U8, align_bytes=64, name="adj_scales")
+            nc.vector.quantize_mx(
+                out=adj_codes[unit][:].bitcast(FP8X4), scales=adj_scales[unit][:], in_=adj_grouped[unit][:]
+            )
+
+        def multiply_agg(unit):
+            for gi, g in enumerate(graphs_of(unit)):
+                nodes = slice(gi * P, (gi + 1) * P)
+                agg_bank[unit, gi] = psum_agg.tile([P, FEAT_TILES, P], F32, name="agg_bank")
+                for t in range(FEAT_TILES):
+                    feats = slice(t * P, (t + 1) * P)
+                    nc.tensor.matmul_mx(
+                        out=agg_bank[unit, gi][:, t, :],
+                        lhsT=x_codes[g][:, feats].bitcast(FP8X4),
+                        lhsT_scale=x_scales[g][:, feats],
+                        rhs=adj_codes[unit][:, nodes].bitcast(FP8X4),
+                        rhs_scale=adj_scales[unit][:, nodes],
+                        start=True,
+                        stop=True,
+                    )
+
+        def copy_agg_out(unit):
+            agg_grouped[unit] = hand_over.tile([P, PAIR, P, PACK], BF16, align_bytes=64, name="agg_grouped")
+            for gi in range(PAIR):
+                nc.scalar.copy(
+                    out=agg_grouped[unit][:, gi, :, :], in_=agg_bank[unit, gi][:].rearrange("c t n -> c n t")
+                )
+
+        def quantise_agg(unit):
+            agg_codes[unit] = hand_over.tile([P, PAIR * P], U32, align_bytes=64, name="agg_codes")
+            agg_scales[unit] = hand_over.tile([P, PAIR * P], U8, align_bytes=64, name="agg_scales")
+            nc.vector.quantize_mx(
+                out=agg_codes[unit][:].bitcast(FP8X4),
+                scales=agg_scales[unit][:],
+                in_=agg_grouped[unit][:].rearrange("c g n t -> c (g n t)"),
+            )
+
+        def multiply_h(unit):
+            h_bank[unit] = psum_h.tile([P, PAIR, OUTS], F32, name="h_bank")
+            for gi in range(PAIR):
+                nodes = slice(gi * P, (gi + 1) * P)
+                nc.tensor.matmul_mx(
+                    out=h_bank[unit][:, gi, :],
+                    lhsT=agg_codes[unit][:, nodes].bitcast(FP8X4),
+                    lhsT_scale=agg_scales[unit][:, nodes],
+                    rhs=w_codes[:].bitcast(FP8X4),
+                    rhs_scale=w_scales[:],
+                    start=True,
+                    stop=True,
+                )
+
+        def add_bias(unit):
+            h_sb[unit] = hand_over.tile([P, PAIR, OUTS], F32, name="h_sb")
+            nc.vector.tensor_tensor(out=h_sb[unit][:], in0=h_bank[unit][:], in1=bias[:], op=ALU.add)
+
+        def relu_and_square_sum(unit):
+            node_tile = unit // GROUPS
+            if unit % GROUPS == 0:
+                square_sum[node_tile] = per_node_tile.tile([P, GRAPHS], F32, name="square_sum")
+                relu_stats[node_tile] = per_node_tile.tile([P, GRAPHS, BN_FIELDS], F32, name="relu_stats")
+            result[unit] = result_pool.tile([P, PAIR, OUTS], F32, name="result")
+            nc.vector.tensor_scalar_max(out=result[unit][:], in0=h_sb[unit][:], scalar1=0.0)
+            for gi, g in enumerate(graphs_of(unit)):
+                squares = unread_pool.tile([P, OUTS], F32, name="squares")
+                nc.scalar.activation(
+                    out=squares[:],
+                    in_=h_sb[unit][:, gi, :],
+                    func=ACT.Square,
+                    accum_out=square_sum[node_tile][:, g : g + 1],
+                )
+
+        def relu_statistics(unit):
+            node_tile = unit // GROUPS
+            for gi, g in enumerate(graphs_of(unit)):
+                nc.vector.bn_stats(out=relu_stats[node_tile][:, g, :], in_=result[unit][:, gi, :])
+
+        def norms(unit):
+            if unit % GROUPS != GROUPS - 1:
+                return
+            node_tile = unit // GROUPS
+            clamped = per_node_tile.tile([P, GRAPHS], F32, name="clamped")
+            nc.vector.tensor_scalar_max(out=clamped[:], in0=square_sum[node_tile][:], scalar1=NORM_EPS * NORM_EPS)
+            norm[node_tile] = per_node_tile.tile([P, GRAPHS], F32, name="norm")
+            nc.scalar.sqrt(out=norm[node_tile][:], in_=clamped[:])
+
+        def moments(unit):
+            if unit % GROUPS != GROUPS - 1:
+                return
+            node_tile = unit // GROUPS
+            inverse_norm[node_tile] = per_node_tile.tile([P, GRAPHS], F32, name="inverse_norm")
+            inverse = inverse_norm[node_tile]
+            nc.vector.reciprocal(out=inverse[:], in_=norm[node_tile][:])
+            inverse_square = per_node_tile.tile([P, GRAPHS], F32, name="inverse_square")
+            nc.vector.tensor_tensor(out=inverse_square[:], in0=inverse[:], in1=inverse[:], op=ALU.mult)
+            triples = relu_stats[node_tile][:].rearrange("p g (h s) -> p g h s", s=3)
+            nc.vector.tensor_tensor(
+                out=triples[:, :, :, 1],
+                in0=triples[:, :, :, 1],
+                in1=inverse[:].unsqueeze(2).to_broadcast([P, GRAPHS, 2]),
+                op=ALU.mult,
+            )
+            nc.vector.tensor_tensor(
+                out=triples[:, :, :, 2],
+                in0=triples[:, :, :, 2],
+                in1=inverse_square[:].unsqueeze(2).to_broadcast([P, GRAPHS, 2]),
+                op=ALU.mult,
+            )
+            mean_var[node_tile] = per_node_tile.tile([P, 2], F32, name="mean_var")
+            nc.vector.bn_aggr(out=mean_var[node_tile][:], in_=relu_stats[node_tile][:].rearrange("p g s -> p (g s)"))
+            padded = per_node_tile.tile([P, 1], F32, name="padded")
+            nc.vector.tensor_scalar_add(out=padded[:], in0=mean_var[node_tile][:, 1:2], scalar1=BN_EPS)
+            deviation[node_tile] = per_node_tile.tile([P, 1], F32, name="deviation")
+            nc.scalar.sqrt(out=deviation[node_tile][:], in_=padded[:])
+
+        def factors(unit):
+            if unit % GROUPS != GROUPS - 1:
+                return
+            node_tile = unit // GROUPS
+            inverse_deviation = per_node_tile.tile([P, 1], F32, name="inverse_deviation")
+            nc.vector.reciprocal(out=inverse_deviation[:], in_=deviation[node_tile][:])
+            factor[node_tile] = per_node_tile.tile([P, GRAPHS], F32, name="factor")
+            nc.vector.tensor_scalar_mul(
+                out=factor[node_tile][:], in0=inverse_norm[node_tile][:], scalar1=inverse_deviation[:, 0:1]
+            )
+            shift[node_tile] = per_node_tile.tile([P, 1], F32, name="shift")
+            nc.vector.tensor_scalar(
+                out=shift[node_tile][:],
+                in0=mean_var[node_tile][:, 0:1],
+                scalar1=inverse_deviation[:, 0:1],
+                scalar2=-1.0,
+                op0=ALU.mult,
+                op1=ALU.mult,
+            )
+
+        def apply(unit):
+            node_tile = unit // GROUPS
+            for gi, g in enumerate(graphs_of(unit)):
+                nc.vector.tensor_scalar(
+                    out=result[unit][:, gi, :],
+                    in0=result[unit][:, gi, :],
+                    scalar1=factor[node_tile][:, g : g + 1],
+                    scalar2=shift[node_tile][:, 0:1],
+                    op0=ALU.mult,
+                    op1=ALU.add,
+                )
+
+        def store(unit):
+            node_tile = unit // GROUPS
+            first = graphs_of(unit)[0]
+            nc.sync.dma_start(out=out_rows[:, first : first + PAIR, node_tile, :], in_=result[unit][:])
+
+        def run(stage, unit):
+            if 0 <= unit < UNITS:
+                stage(unit)
+
+        for step in range(UNITS + LAG_STORE):
+            run(store, step - LAG_STORE)
+            run(apply, step - LAG_APPLY)
+            run(factors, step - LAG_FACTORS)
+            run(moments, step - LAG_MOMENTS)
+            run(norms, step - LAG_NORMS)
+            run(relu_statistics, step - LAG_BN)
+            run(relu_and_square_sum, step - LAG_RELU)
+            run(add_bias, step - LAG_BIAS)
+            run(multiply_h, step - LAG_H)
+            run(quantise_agg, step - LAG_AGG_QUANT)
+            run(copy_agg_out, step - LAG_AGG_OUT)
+            run(multiply_agg, step - LAG_AGG)
+            run(quantise_adj, step - LAG_ADJ_QUANT)
+            run(copy_adj_out, step - LAG_ADJ_OUT)
+            run(transpose_adj, step - LAG_TRANSPOSE)
+            run(quantise_x, step - LAG_X_QUANT)
+            run(regroup_x, step - LAG_X_REGROUP)
+            run(load, step - LAG_LOAD)

@@ -38,9 +38,9 @@ LAG_H = 9
 LAG_BIAS = 10
 LAG_RELU = 11
 LAG_BN = 12
-LAG_NORMS = 13
-LAG_MOMENTS = 14
-LAG_FACTORS = 15
+LAG_NORMS = 12
+LAG_MOMENTS = 13
+LAG_FACTORS = 14
 LAG_APPLY = LAG_FACTORS + GROUPS
 LAG_STORE = LAG_APPLY + 1
 
@@ -48,8 +48,6 @@ LAG_STORE = LAG_APPLY + 1
 def tile_routingassignment_pa_t_kernel(tc, x, adj, W, b, out):
     nc = tc.nc
     with ExitStack() as ctx:
-        ctx.enter_context(tc.manual_schedule())
-
         def pool(name, bufs):
             return ctx.enter_context(tc.tile_pool(name=name, bufs=bufs))
 
@@ -57,7 +55,7 @@ def tile_routingassignment_pa_t_kernel(tc, x, adj, W, b, out):
         x_raw_pool = pool("x_raw", PAIR * (LAG_X_REGROUP - LAG_LOAD + 1))
         x_grouped_pool = pool("x_grouped", PAIR * (LAG_X_QUANT - LAG_X_REGROUP + 1))
         adj_raw_pool = pool("adj_raw", LAG_TRANSPOSE - LAG_LOAD + 1)
-        hand_over = pool("hand_over", 2)
+        hand_over = pool("hand_over", 3)
         result_pool = pool("result", LAG_STORE - LAG_RELU + 1)
         unread_pool = pool("unread", 4)
         per_node_tile = pool("per_node_tile", 2)
@@ -81,7 +79,7 @@ def tile_routingassignment_pa_t_kernel(tc, x, adj, W, b, out):
 
         one = keep.tile([P, 1], F32)
         nc.gpsimd.memset(one[:], 1.0)
-        nc.scalar.sqrt(out=one[:], in_=one[:])
+        nc.scalar.activation(out=one[:], in_=one[:], func=ACT.Abs_reciprocal_sqrt)
 
         w_grouped = keep.tile([P, OUTS, PACK], BF16, align_bytes=64)
         nc.vector.tensor_copy(out=w_grouped[:], in_=w_raw[:].rearrange("c t k -> c k t"))
@@ -104,7 +102,8 @@ def tile_routingassignment_pa_t_kernel(tc, x, adj, W, b, out):
         adj_raw, word_bank, adj_grouped, adj_codes, adj_scales = {}, {}, {}, {}, {}
         agg_bank, agg_grouped, agg_codes, agg_scales = {}, {}, {}, {}
         h_bank, h_sb, result = {}, {}, {}
-        square_sum, relu_stats, norm, inverse_norm, mean_var, deviation, factor, shift = {}, {}, {}, {}, {}, {}, {}, {}
+        square_sum, relu_stats, inverse_norm, inverse_square = {}, {}, {}, {}
+        mean_var, inverse_deviation, factor, shift = {}, {}, {}, {}
 
         def graphs_of(unit):
             first = (unit % GROUPS) * PAIR
@@ -248,55 +247,62 @@ def tile_routingassignment_pa_t_kernel(tc, x, adj, W, b, out):
             if unit % GROUPS != GROUPS - 1:
                 return
             node_tile = unit // GROUPS
+            inverse_norm[node_tile] = per_node_tile.tile([P, GRAPHS], F32, name="inverse_norm")
+            nc.scalar.activation(
+                out=inverse_norm[node_tile][:], in_=square_sum[node_tile][:], func=ACT.Abs_reciprocal_sqrt
+            )
             clamped = per_node_tile.tile([P, GRAPHS], F32, name="clamped")
             nc.vector.tensor_scalar_max(out=clamped[:], in0=square_sum[node_tile][:], scalar1=NORM_EPS * NORM_EPS)
-            norm[node_tile] = per_node_tile.tile([P, GRAPHS], F32, name="norm")
-            nc.scalar.sqrt(out=norm[node_tile][:], in_=clamped[:])
+            inverse_square[node_tile] = per_node_tile.tile([P, GRAPHS], F32, name="inverse_square")
+            nc.vector.reciprocal(out=inverse_square[node_tile][:], in_=clamped[:])
 
         def moments(unit):
             if unit % GROUPS != GROUPS - 1:
                 return
             node_tile = unit // GROUPS
-            inverse_norm[node_tile] = per_node_tile.tile([P, GRAPHS], F32, name="inverse_norm")
-            inverse = inverse_norm[node_tile]
-            nc.vector.reciprocal(out=inverse[:], in_=norm[node_tile][:])
-            inverse_square = per_node_tile.tile([P, GRAPHS], F32, name="inverse_square")
-            nc.vector.tensor_tensor(out=inverse_square[:], in0=inverse[:], in1=inverse[:], op=ALU.mult)
             triples = relu_stats[node_tile][:].rearrange("p g (h s) -> p g h s", s=3)
-            nc.vector.tensor_tensor(
-                out=triples[:, :, :, 1],
-                in0=triples[:, :, :, 1],
-                in1=inverse[:].unsqueeze(2).to_broadcast([P, GRAPHS, 2]),
-                op=ALU.mult,
-            )
             nc.vector.tensor_tensor(
                 out=triples[:, :, :, 2],
                 in0=triples[:, :, :, 2],
-                in1=inverse_square[:].unsqueeze(2).to_broadcast([P, GRAPHS, 2]),
+                in1=inverse_square[node_tile][:].unsqueeze(2).to_broadcast([P, GRAPHS, 2]),
                 op=ALU.mult,
+            )
+            nc.vector.scalar_tensor_tensor(
+                out=triples[:, :, :, 1],
+                in0=inverse_norm[node_tile][:].unsqueeze(2).to_broadcast([P, GRAPHS, 2]),
+                scalar=1.0 / NORM_EPS,
+                in1=triples[:, :, :, 1],
+                op0=ALU.min,
+                op1=ALU.mult,
             )
             mean_var[node_tile] = per_node_tile.tile([P, 2], F32, name="mean_var")
             nc.vector.bn_aggr(out=mean_var[node_tile][:], in_=relu_stats[node_tile][:].rearrange("p g s -> p (g s)"))
-            padded = per_node_tile.tile([P, 1], F32, name="padded")
-            nc.vector.tensor_scalar_add(out=padded[:], in0=mean_var[node_tile][:, 1:2], scalar1=BN_EPS)
-            deviation[node_tile] = per_node_tile.tile([P, 1], F32, name="deviation")
-            nc.scalar.sqrt(out=deviation[node_tile][:], in_=padded[:])
+            inverse_deviation[node_tile] = per_node_tile.tile([P, 1], F32, name="inverse_deviation")
+            nc.scalar.activation(
+                out=inverse_deviation[node_tile][:],
+                in_=mean_var[node_tile][:, 1:2],
+                func=ACT.Abs_reciprocal_sqrt,
+                bias=BN_EPS,
+            )
 
         def factors(unit):
             if unit % GROUPS != GROUPS - 1:
                 return
             node_tile = unit // GROUPS
-            inverse_deviation = per_node_tile.tile([P, 1], F32, name="inverse_deviation")
-            nc.vector.reciprocal(out=inverse_deviation[:], in_=deviation[node_tile][:])
             factor[node_tile] = per_node_tile.tile([P, GRAPHS], F32, name="factor")
-            nc.vector.tensor_scalar_mul(
-                out=factor[node_tile][:], in0=inverse_norm[node_tile][:], scalar1=inverse_deviation[:, 0:1]
+            nc.vector.tensor_scalar(
+                out=factor[node_tile][:],
+                in0=inverse_norm[node_tile][:],
+                scalar1=1.0 / NORM_EPS,
+                scalar2=inverse_deviation[node_tile][:, 0:1],
+                op0=ALU.min,
+                op1=ALU.mult,
             )
             shift[node_tile] = per_node_tile.tile([P, 1], F32, name="shift")
             nc.vector.tensor_scalar(
                 out=shift[node_tile][:],
                 in0=mean_var[node_tile][:, 0:1],
-                scalar1=inverse_deviation[:, 0:1],
+                scalar1=inverse_deviation[node_tile][:, 0:1],
                 scalar2=-1.0,
                 op0=ALU.mult,
                 op1=ALU.mult,

@@ -19,28 +19,28 @@ FEAT_TILES = FEATS // P
 PAIR = 2
 GROUPS = GRAPHS // PAIR
 UNITS = NODE_TILES * GROUPS
-BN_FIELDS = 6
+TRIPLE = 3
 BN_EPS = 1e-5
 NORM_EPS = 1e-12
 
 FLOPS = 2 * GRAPHS * NODES * NODES * FEATS + 2 * GRAPHS * NODES * FEATS * OUTS
 
 LAG_LOAD = 0
-LAG_X_REGROUP = 2
-LAG_X_QUANT = 3
-LAG_TRANSPOSE = 3
-LAG_ADJ_OUT = 4
-LAG_ADJ_QUANT = 5
-LAG_AGG = 6
-LAG_AGG_OUT = 7
-LAG_AGG_QUANT = 8
-LAG_H = 9
-LAG_BIAS = 10
-LAG_RELU = 11
-LAG_BN = 12
-LAG_NORMS = 12
-LAG_MOMENTS = 13
-LAG_FACTORS = 14
+LAG_X_REGROUP = LAG_LOAD + 3
+LAG_X_QUANT = LAG_X_REGROUP + 1
+LAG_TRANSPOSE = LAG_LOAD + 3
+LAG_ADJ_OUT = LAG_TRANSPOSE + 1
+LAG_ADJ_QUANT = LAG_ADJ_OUT + 1
+LAG_AGG = LAG_ADJ_QUANT + 1
+LAG_AGG_OUT = LAG_AGG + 1
+LAG_AGG_QUANT = LAG_AGG_OUT + 1
+LAG_H = LAG_AGG_QUANT + 1
+LAG_BIAS = LAG_H + 1
+LAG_RELU = LAG_BIAS + 1
+LAG_STATS = LAG_RELU + 1
+LAG_NORMS = LAG_RELU + 1
+LAG_MOMENTS = LAG_STATS + 1
+LAG_FACTORS = LAG_MOMENTS + 1
 LAG_APPLY = LAG_FACTORS + GROUPS
 LAG_STORE = LAG_APPLY + 1
 
@@ -48,6 +48,7 @@ LAG_STORE = LAG_APPLY + 1
 def tile_routingassignment_pa_t_kernel(tc, x, adj, W, b, out):
     nc = tc.nc
     with ExitStack() as ctx:
+
         def pool(name, bufs):
             return ctx.enter_context(tc.tile_pool(name=name, bufs=bufs))
 
@@ -67,36 +68,12 @@ def tile_routingassignment_pa_t_kernel(tc, x, adj, W, b, out):
         adj_rows = adj.rearrange("g (p t) m -> p g t m", t=NODE_TILES)
         out_rows = out.rearrange("g (p t) k -> p g t k", t=NODE_TILES)
 
-        w_raw = keep.tile([P, FEAT_TILES, OUTS], BF16)
-        nc.scalar.dma_start(out=w_raw[:], in_=W.rearrange("(t c) k -> c t k", t=FEAT_TILES))
-        bias_row = keep.tile([P, OUTS], BF16)
-        nc.gpsimd.memset(bias_row[:], 0.0)
-        nc.scalar.dma_start(out=bias_row[0:1, :], in_=b.rearrange("(o k) -> o k", o=1))
-        ones = keep.tile([P, P], BF16)
-        nc.gpsimd.memset(ones[:], 1.0)
-        identity = keep.tile([P, P], F32)
-        make_identity(nc, identity[:])
-
-        one = keep.tile([P, 1], F32)
-        nc.gpsimd.memset(one[:], 1.0)
-        nc.scalar.activation(out=one[:], in_=one[:], func=ACT.Abs_reciprocal_sqrt)
-
-        w_grouped = keep.tile([P, OUTS, PACK], BF16, align_bytes=64)
-        nc.vector.tensor_copy(out=w_grouped[:], in_=w_raw[:].rearrange("c t k -> c k t"))
-        w_codes = keep.tile([P, OUTS], U32, align_bytes=64)
-        w_scales = keep.tile([P, OUTS], U8, align_bytes=64)
-        nc.vector.quantize_mx(
-            out=w_codes[:].bitcast(FP8X4), scales=w_scales[:], in_=w_grouped[:].rearrange("c k t -> c (k t)")
-        )
-
-        bias_bank = psum_h.tile([P, PAIR, OUTS], F32, name="h_bank")
-        nc.tensor.matmul(out=bias_bank[:, 0, :], lhsT=ones[:], rhs=bias_row[:], start=True, stop=True)
-        bias = keep.tile([P, PAIR, OUTS], F32)
-        for gi in range(PAIR):
-            nc.vector.tensor_copy(out=bias[:, gi, :], in_=bias_bank[:, 0, :])
-
         x_codes = [keep.tile([P, FEATS], U32, align_bytes=64, name="x_codes%d" % g) for g in range(GRAPHS)]
         x_scales = [keep.tile([P, FEATS], U8, align_bytes=64, name="x_scales%d" % g) for g in range(GRAPHS)]
+        w_codes = keep.tile([P, OUTS], U32, align_bytes=64)
+        w_scales = keep.tile([P, OUTS], U8, align_bytes=64)
+        bias = keep.tile([P, PAIR, OUTS], F32)
+        identity = keep.tile([P, P], F32)
 
         x_raw, x_grouped = {}, {}
         adj_raw, word_bank, adj_grouped, adj_codes, adj_scales = {}, {}, {}, {}, {}
@@ -108,6 +85,34 @@ def tile_routingassignment_pa_t_kernel(tc, x, adj, W, b, out):
         def graphs_of(unit):
             first = (unit % GROUPS) * PAIR
             return range(first, first + PAIR)
+
+        def is_last_of_node_tile(unit):
+            return unit % GROUPS == GROUPS - 1
+
+        def prepare_constants():
+            w_raw = keep.tile([P, FEAT_TILES, OUTS], BF16)
+            nc.scalar.dma_start(out=w_raw[:], in_=W.rearrange("(t c) k -> c t k", t=FEAT_TILES))
+            bias_row = keep.tile([P, OUTS], BF16)
+            nc.gpsimd.memset(bias_row[:], 0.0)
+            nc.scalar.dma_start(out=bias_row[0:1, :], in_=b.rearrange("(o k) -> o k", o=1))
+            ones = keep.tile([P, P], BF16)
+            nc.gpsimd.memset(ones[:], 1.0)
+            make_identity(nc, identity[:])
+
+            one = keep.tile([P, 1], F32)
+            nc.gpsimd.memset(one[:], 1.0)
+            nc.scalar.activation(out=one[:], in_=one[:], func=ACT.Abs_reciprocal_sqrt)
+
+            w_grouped = keep.tile([P, OUTS, PACK], BF16, align_bytes=64)
+            nc.vector.tensor_copy(out=w_grouped[:], in_=w_raw[:].rearrange("c t k -> c k t"))
+            nc.vector.quantize_mx(
+                out=w_codes[:].bitcast(FP8X4), scales=w_scales[:], in_=w_grouped[:].rearrange("c k t -> c (k t)")
+            )
+
+            bias_bank = psum_h.tile([P, PAIR, OUTS], F32, name="h_bank")
+            nc.tensor.matmul(out=bias_bank[:, 0, :], lhsT=ones[:], rhs=bias_row[:], start=True, stop=True)
+            for gi in range(PAIR):
+                nc.vector.tensor_copy(out=bias[:, gi, :], in_=bias_bank[:, 0, :])
 
         def load(unit):
             node_tile = unit // GROUPS
@@ -226,7 +231,7 @@ def tile_routingassignment_pa_t_kernel(tc, x, adj, W, b, out):
             node_tile = unit // GROUPS
             if unit % GROUPS == 0:
                 square_sum[node_tile] = per_node_tile.tile([P, GRAPHS], F32, name="square_sum")
-                relu_stats[node_tile] = per_node_tile.tile([P, GRAPHS, BN_FIELDS], F32, name="relu_stats")
+                relu_stats[node_tile] = per_node_tile.tile([P, GRAPHS, TRIPLE], F32, name="relu_stats")
             result[unit] = result_pool.tile([P, PAIR, OUTS], F32, name="result")
             nc.vector.tensor_scalar_max(out=result[unit][:], in0=h_sb[unit][:], scalar1=0.0)
             for gi, g in enumerate(graphs_of(unit)):
@@ -239,12 +244,14 @@ def tile_routingassignment_pa_t_kernel(tc, x, adj, W, b, out):
                 )
 
         def relu_statistics(unit):
-            node_tile = unit // GROUPS
-            for gi, g in enumerate(graphs_of(unit)):
-                nc.vector.bn_stats(out=relu_stats[node_tile][:, g, :], in_=result[unit][:, gi, :])
+            first = graphs_of(unit)[0]
+            nc.vector.bn_stats(
+                out=relu_stats[unit // GROUPS][:, first : first + PAIR, :].rearrange("p g s -> p (g s)"),
+                in_=result[unit][:].rearrange("p g k -> p k g"),
+            )
 
         def norms(unit):
-            if unit % GROUPS != GROUPS - 1:
+            if not is_last_of_node_tile(unit):
                 return
             node_tile = unit // GROUPS
             inverse_norm[node_tile] = per_node_tile.tile([P, GRAPHS], F32, name="inverse_norm")
@@ -257,26 +264,23 @@ def tile_routingassignment_pa_t_kernel(tc, x, adj, W, b, out):
             nc.vector.reciprocal(out=inverse_square[node_tile][:], in_=clamped[:])
 
         def moments(unit):
-            if unit % GROUPS != GROUPS - 1:
+            if not is_last_of_node_tile(unit):
                 return
             node_tile = unit // GROUPS
-            triples = relu_stats[node_tile][:].rearrange("p g (h s) -> p g h s", s=3)
+            triples = relu_stats[node_tile]
             nc.vector.tensor_tensor(
-                out=triples[:, :, :, 2],
-                in0=triples[:, :, :, 2],
-                in1=inverse_square[node_tile][:].unsqueeze(2).to_broadcast([P, GRAPHS, 2]),
-                op=ALU.mult,
+                out=triples[:, :, 2], in0=triples[:, :, 2], in1=inverse_square[node_tile][:], op=ALU.mult
             )
             nc.vector.scalar_tensor_tensor(
-                out=triples[:, :, :, 1],
-                in0=inverse_norm[node_tile][:].unsqueeze(2).to_broadcast([P, GRAPHS, 2]),
+                out=triples[:, :, 1],
+                in0=inverse_norm[node_tile][:],
                 scalar=1.0 / NORM_EPS,
-                in1=triples[:, :, :, 1],
+                in1=triples[:, :, 1],
                 op0=ALU.min,
                 op1=ALU.mult,
             )
             mean_var[node_tile] = per_node_tile.tile([P, 2], F32, name="mean_var")
-            nc.vector.bn_aggr(out=mean_var[node_tile][:], in_=relu_stats[node_tile][:].rearrange("p g s -> p (g s)"))
+            nc.vector.bn_aggr(out=mean_var[node_tile][:], in_=triples[:].rearrange("p g s -> p (g s)"))
             inverse_deviation[node_tile] = per_node_tile.tile([P, 1], F32, name="inverse_deviation")
             nc.scalar.activation(
                 out=inverse_deviation[node_tile][:],
@@ -286,7 +290,7 @@ def tile_routingassignment_pa_t_kernel(tc, x, adj, W, b, out):
             )
 
         def factors(unit):
-            if unit % GROUPS != GROUPS - 1:
+            if not is_last_of_node_tile(unit):
                 return
             node_tile = unit // GROUPS
             factor[node_tile] = per_node_tile.tile([P, GRAPHS], F32, name="factor")
@@ -308,7 +312,7 @@ def tile_routingassignment_pa_t_kernel(tc, x, adj, W, b, out):
                 op1=ALU.mult,
             )
 
-        def apply(unit):
+        def scale_and_shift(unit):
             node_tile = unit // GROUPS
             for gi, g in enumerate(graphs_of(unit)):
                 nc.vector.tensor_scalar(
@@ -321,9 +325,8 @@ def tile_routingassignment_pa_t_kernel(tc, x, adj, W, b, out):
                 )
 
         def store(unit):
-            node_tile = unit // GROUPS
             first = graphs_of(unit)[0]
-            nc.sync.dma_start(out=out_rows[:, first : first + PAIR, node_tile, :], in_=result[unit][:])
+            nc.sync.dma_start(out=out_rows[:, first : first + PAIR, unit // GROUPS, :], in_=result[unit][:])
 
         def run(stage, unit):
             if 0 <= unit < UNITS:
@@ -331,11 +334,11 @@ def tile_routingassignment_pa_t_kernel(tc, x, adj, W, b, out):
 
         for step in range(UNITS + LAG_STORE):
             run(store, step - LAG_STORE)
-            run(apply, step - LAG_APPLY)
+            run(scale_and_shift, step - LAG_APPLY)
             run(factors, step - LAG_FACTORS)
             run(moments, step - LAG_MOMENTS)
             run(norms, step - LAG_NORMS)
-            run(relu_statistics, step - LAG_BN)
+            run(relu_statistics, step - LAG_STATS)
             run(relu_and_square_sum, step - LAG_RELU)
             run(add_bias, step - LAG_BIAS)
             run(multiply_h, step - LAG_H)
@@ -348,3 +351,5 @@ def tile_routingassignment_pa_t_kernel(tc, x, adj, W, b, out):
             run(quantise_x, step - LAG_X_QUANT)
             run(regroup_x, step - LAG_X_REGROUP)
             run(load, step - LAG_LOAD)
+            if step == 0:
+                prepare_constants()

from contextlib import ExitStack

import concourse.mybir as mybir
from concourse.masks import make_identity

F32 = mybir.dt.float32
BF16 = mybir.dt.bfloat16
U32 = mybir.dt.uint32
U8 = mybir.dt.uint8
FP8X4 = mybir.dt.float8_e4m3fn_x4
ALU = mybir.AluOpType
ACT = mybir.ActivationFunctionType

P = 128
PACK = 4
GRAPHS, NODES, FEATS, OUTS = 16, 512, 512, 256
NODE_TILES = NODES // P
FEAT_TILES = FEATS // P
PAIR = 2
GROUPS = GRAPHS // PAIR
UNITS = NODE_TILES * GROUPS
TRIPLE = 3
BN_EPS = 1e-5
NORM_EPS = 1e-12

FLOPS = 2 * GRAPHS * NODES * NODES * FEATS + 2 * GRAPHS * NODES * FEATS * OUTS

LAG_LOAD = 0
LAG_X_REGROUP = LAG_LOAD + 3
LAG_X_QUANT = LAG_X_REGROUP + 1
LAG_TRANSPOSE = LAG_LOAD + 3
LAG_ADJ_OUT = LAG_TRANSPOSE + 1
LAG_ADJ_QUANT = LAG_ADJ_OUT + 1
LAG_AGG = LAG_ADJ_QUANT + 1
LAG_AGG_OUT = LAG_AGG + 1
LAG_AGG_QUANT = LAG_AGG_OUT + 1
LAG_H = LAG_AGG_QUANT + 1
LAG_BIAS = LAG_H + 1
LAG_RELU = LAG_BIAS + 1
LAG_STATS = LAG_RELU + 1
LAG_NORMS = LAG_RELU + 1
LAG_MOMENTS = LAG_STATS + 1
LAG_FACTORS = LAG_MOMENTS + 1
LAG_APPLY = LAG_FACTORS + GROUPS
LAG_STORE = LAG_APPLY + 1


def tile_routingassignment_pa_t_kernel(tc, x, adj, W, b, out):
    nc = tc.nc
    with ExitStack() as ctx:

        def pool(name, bufs):
            return ctx.enter_context(tc.tile_pool(name=name, bufs=bufs))

        keep = pool("keep", 1)
        x_raw_pool = pool("x_raw", PAIR * (LAG_X_REGROUP - LAG_LOAD + 1))
        x_grouped_pool = pool("x_grouped", PAIR * (LAG_X_QUANT - LAG_X_REGROUP + 1))
        adj_raw_pool = pool("adj_raw", LAG_TRANSPOSE - LAG_LOAD + 1)
        hand_over = pool("hand_over", 3)
        result_pool = pool("result", LAG_STORE - LAG_RELU + 1)
        unread_pool = pool("unread", 4)
        per_node_tile = pool("per_node_tile", 2)
        psum_words = ctx.enter_context(tc.psum_pool(name="psum_words", bufs=2))
        psum_agg = ctx.enter_context(tc.psum_pool(name="psum_agg", bufs=2 * PAIR))
        psum_h = ctx.enter_context(tc.psum_pool(name="psum_h", bufs=2))

        x_rows = x.rearrange("g (u q e) f -> g q u (e f)", u=2, e=2)
        adj_rows = adj.rearrange("g (p t) m -> p g t m", t=NODE_TILES)
        out_rows = out.rearrange("g (p t) k -> p g t k", t=NODE_TILES)

        x_codes = [keep.tile([P, FEATS], U32, align_bytes=64, name="x_codes%d" % g) for g in range(GRAPHS)]
        x_scales = [keep.tile([P, FEATS], U8, align_bytes=64, name="x_scales%d" % g) for g in range(GRAPHS)]
        w_codes = keep.tile([P, OUTS], U32, align_bytes=64)
        w_scales = keep.tile([P, OUTS], U8, align_bytes=64)
        bias = keep.tile([P, PAIR, OUTS], F32)
        identity = keep.tile([P, P], F32)

        x_raw, x_grouped = {}, {}
        adj_raw, word_bank, adj_grouped, adj_codes, adj_scales = {}, {}, {}, {}, {}
        agg_bank, agg_grouped, agg_codes, agg_scales = {}, {}, {}, {}
        h_bank, h_sb, result = {}, {}, {}
        square_sum, relu_stats, inverse_norm, inverse_square = {}, {}, {}, {}
        mean_var, inverse_deviation, factor, shift = {}, {}, {}, {}

        def graphs_of(unit):
            first = (unit % GROUPS) * PAIR
            return range(first, first + PAIR)

        def is_last_of_node_tile(unit):
            return unit % GROUPS == GROUPS - 1

        def prepare_constants():
            w_raw = keep.tile([P, FEAT_TILES, OUTS], BF16)
            nc.scalar.dma_start(out=w_raw[:], in_=W.rearrange("(t c) k -> c t k", t=FEAT_TILES))
            bias_row = keep.tile([P, OUTS], BF16)
            nc.gpsimd.memset(bias_row[:], 0.0)
            nc.scalar.dma_start(out=bias_row[0:1, :], in_=b.rearrange("(o k) -> o k", o=1))
            ones = keep.tile([P, P], BF16)
            nc.gpsimd.memset(ones[:], 1.0)
            make_identity(nc, identity[:])

            one = keep.tile([P, 1], F32)
            nc.gpsimd.memset(one[:], 1.0)
            nc.scalar.activation(out=one[:], in_=one[:], func=ACT.Abs_reciprocal_sqrt)

            w_grouped = keep.tile([P, OUTS, PACK], BF16, align_bytes=64)
            nc.vector.tensor_copy(out=w_grouped[:], in_=w_raw[:].rearrange("c t k -> c k t"))
            nc.vector.quantize_mx(
                out=w_codes[:].bitcast(FP8X4), scales=w_scales[:], in_=w_grouped[:].rearrange("c k t -> c (k t)")
            )

            bias_bank = psum_h.tile([P, PAIR, OUTS], F32, name="h_bank")
            nc.tensor.matmul(out=bias_bank[:, 0, :], lhsT=ones[:], rhs=bias_row[:], start=True, stop=True)
            for gi in range(PAIR):
                nc.vector.tensor_copy(out=bias[:, gi, :], in_=bias_bank[:, 0, :])

        def load(unit):
            node_tile = unit // GROUPS
            graphs = graphs_of(unit)
            if node_tile == 0:
                for g in graphs:
                    x_raw[g] = x_raw_pool.tile([P, 2, 2 * FEATS], BF16, name="x_raw")
                    nc.sync.dma_start(out=x_raw[g][:], in_=x_rows[g])
            adj_raw[unit] = adj_raw_pool.tile([P, PAIR * NODES], BF16, name="adj_raw")
            nc.sync.dma_start(
                out=adj_raw[unit][:].rearrange("p (g m) -> p g m", g=PAIR),
                in_=adj_rows[:, graphs[0] : graphs[0] + PAIR, node_tile, :],
            )

        def regroup_x(unit):
            if unit >= GROUPS:
                return
            half = FEATS // 2
            for g in graphs_of(unit):
                x_grouped[g] = x_grouped_pool.tile([P, FEATS, PACK], BF16, align_bytes=64, name="x_grouped")
                rows = x_raw[g][:].rearrange("q u (e f) -> q (u e) f", e=2)
                nc.vector.tensor_copy(
                    out=x_grouped[g][:, 0:half, :].rearrange("q (c i) j -> q c j i", i=4),
                    in_=rows[:, :, 0:half].rearrange("q j (c i) -> q c j i", i=4),
                )
                nc.scalar.copy(
                    out=x_grouped[g][:, half:FEATS, :].rearrange("q (c i) j -> q c j i", i=4),
                    in_=rows[:, :, half:FEATS].rearrange("q j (c i) -> q c j i", i=4),
                )

        def quantise_x(unit):
            if unit >= GROUPS:
                return
            for g in graphs_of(unit):
                nc.vector.quantize_mx(
                    out=x_codes[g][:].bitcast(FP8X4),
                    scales=x_scales[g][:],
                    in_=x_grouped[g][:].rearrange("q f j -> q (f j)"),
                )

        def transpose_adj(unit):
            word_bank[unit] = psum_words.tile([P, PAIR, 2, P], F32, name="word_bank")
            words = adj_raw[unit][:].bitcast(F32)
            for gi in range(PAIR):
                for u in range(2):
                    first = (gi * 2 + u) * P
                    nc.tensor.transpose(
                        out=word_bank[unit][:, gi, u, :], in_=words[:, first : first + P], identity=identity[:]
                    )

        def copy_adj_out(unit):
            adj_grouped[unit] = hand_over.tile([P, PAIR * P * PACK], BF16, align_bytes=64, name="adj_grouped")
            nc.scalar.copy(
                out=adj_grouped[unit][:].bitcast(F32).rearrange("q (g n u) -> q g n u", g=PAIR, u=2),
                in_=word_bank[unit][:].rearrange("q g u n -> q g n u"),
            )

        def quantise_adj(unit):
            adj_codes[unit] = hand_over.tile([P, PAIR * P], U32, align_bytes=64, name="adj_codes")
            adj_scales[unit] = hand_over.tile([P, PAIR * P], U8, align_bytes=64, name="adj_scales")
            nc.vector.quantize_mx(
                out=adj_codes[unit][:].bitcast(FP8X4), scales=adj_scales[unit][:], in_=adj_grouped[unit][:]
            )

        def multiply_agg(unit):
            for gi, g in enumerate(graphs_of(unit)):
                nodes = slice(gi * P, (gi + 1) * P)
                agg_bank[unit, gi] = psum_agg.tile([P, FEAT_TILES, P], F32, name="agg_bank")
                for t in range(FEAT_TILES):
                    feats = slice(t * P, (t + 1) * P)
                    nc.tensor.matmul_mx(
                        out=agg_bank[unit, gi][:, t, :],
                        lhsT=x_codes[g][:, feats].bitcast(FP8X4),
                        lhsT_scale=x_scales[g][:, feats],
                        rhs=adj_codes[unit][:, nodes].bitcast(FP8X4),
                        rhs_scale=adj_scales[unit][:, nodes],
                        start=True,
                        stop=True,
                    )

        def copy_agg_out(unit):
            agg_grouped[unit] = hand_over.tile([P, PAIR, P, PACK], BF16, align_bytes=64, name="agg_grouped")
            for gi in range(PAIR):
                nc.scalar.copy(
                    out=agg_grouped[unit][:, gi, :, :], in_=agg_bank[unit, gi][:].rearrange("c t n -> c n t")
                )

        def quantise_agg(unit):
            agg_codes[unit] = hand_over.tile([P, PAIR * P], U32, align_bytes=64, name="agg_codes")
            agg_scales[unit] = hand_over.tile([P, PAIR * P], U8, align_bytes=64, name="agg_scales")
            nc.vector.quantize_mx(
                out=agg_codes[unit][:].bitcast(FP8X4),
                scales=agg_scales[unit][:],
                in_=agg_grouped[unit][:].rearrange("c g n t -> c (g n t)"),
            )

        def multiply_h(unit):
            h_bank[unit] = psum_h.tile([P, PAIR, OUTS], F32, name="h_bank")
            for gi in range(PAIR):
                nodes = slice(gi * P, (gi + 1) * P)
                nc.tensor.matmul_mx(
                    out=h_bank[unit][:, gi, :],
                    lhsT=agg_codes[unit][:, nodes].bitcast(FP8X4),
                    lhsT_scale=agg_scales[unit][:, nodes],
                    rhs=w_codes[:].bitcast(FP8X4),
                    rhs_scale=w_scales[:],
                    start=True,
                    stop=True,
                )

        def add_bias(unit):
            h_sb[unit] = hand_over.tile([P, PAIR, OUTS], F32, name="h_sb")
            nc.vector.tensor_tensor(out=h_sb[unit][:], in0=h_bank[unit][:], in1=bias[:], op=ALU.add)

        def relu_and_square_sum(unit):
            node_tile = unit // GROUPS
            if unit % GROUPS == 0:
                square_sum[node_tile] = per_node_tile.tile([P, GRAPHS], F32, name="square_sum")
                relu_stats[node_tile] = per_node_tile.tile([P, GRAPHS, TRIPLE], F32, name="relu_stats")
            result[unit] = result_pool.tile([P, PAIR, OUTS], F32, name="result")
            nc.vector.tensor_scalar_max(out=result[unit][:], in0=h_sb[unit][:], scalar1=0.0)
            for gi, g in enumerate(graphs_of(unit)):
                squares = unread_pool.tile([P, OUTS], F32, name="squares")
                nc.scalar.activation(
                    out=squares[:],
                    in_=h_sb[unit][:, gi, :],
                    func=ACT.Square,
                    accum_out=square_sum[node_tile][:, g : g + 1],
                )

        def relu_statistics(unit):
            first = graphs_of(unit)[0]
            nc.vector.bn_stats(
                out=relu_stats[unit // GROUPS][:, first : first + PAIR, :].rearrange("p g s -> p (g s)"),
                in_=result[unit][:].rearrange("p g k -> p k g"),
            )

        def norms(unit):
            if not is_last_of_node_tile(unit):
                return
            node_tile = unit // GROUPS
            inverse_norm[node_tile] = per_node_tile.tile([P, GRAPHS], F32, name="inverse_norm")
            nc.scalar.activation(
                out=inverse_norm[node_tile][:], in_=square_sum[node_tile][:], func=ACT.Abs_reciprocal_sqrt
            )
            clamped = per_node_tile.tile([P, GRAPHS], F32, name="clamped")
            nc.vector.tensor_scalar_max(out=clamped[:], in0=square_sum[node_tile][:], scalar1=NORM_EPS * NORM_EPS)
            inverse_square[node_tile] = per_node_tile.tile([P, GRAPHS], F32, name="inverse_square")
            nc.vector.reciprocal(out=inverse_square[node_tile][:], in_=clamped[:])

        def moments(unit):
            if not is_last_of_node_tile(unit):
                return
            node_tile = unit // GROUPS
            triples = relu_stats[node_tile]
            nc.vector.tensor_tensor(
                out=triples[:, :, 2], in0=triples[:, :, 2], in1=inverse_square[node_tile][:], op=ALU.mult
            )
            nc.vector.scalar_tensor_tensor(
                out=triples[:, :, 1],
                in0=inverse_norm[node_tile][:],
                scalar=1.0 / NORM_EPS,
                in1=triples[:, :, 1],
                op0=ALU.min,
                op1=ALU.mult,
            )
            mean_var[node_tile] = per_node_tile.tile([P, 2], F32, name="mean_var")
            nc.vector.bn_aggr(out=mean_var[node_tile][:], in_=triples[:].rearrange("p g s -> p (g s)"))
            inverse_deviation[node_tile] = per_node_tile.tile([P, 1], F32, name="inverse_deviation")
            nc.scalar.activation(
                out=inverse_deviation[node_tile][:],
                in_=mean_var[node_tile][:, 1:2],
                func=ACT.Abs_reciprocal_sqrt,
                bias=BN_EPS,
            )

        def factors(unit):
            if not is_last_of_node_tile(unit):
                return
            node_tile = unit // GROUPS
            factor[node_tile] = per_node_tile.tile([P, GRAPHS], F32, name="factor")
            nc.vector.tensor_scalar(
                out=factor[node_tile][:],
                in0=inverse_norm[node_tile][:],
                scalar1=1.0 / NORM_EPS,
                scalar2=inverse_deviation[node_tile][:, 0:1],
                op0=ALU.min,
                op1=ALU.mult,
            )
            shift[node_tile] = per_node_tile.tile([P, 1], F32, name="shift")
            nc.vector.tensor_scalar(
                out=shift[node_tile][:],
                in0=mean_var[node_tile][:, 0:1],
                scalar1=inverse_deviation[node_tile][:, 0:1],
                scalar2=-1.0,
                op0=ALU.mult,
                op1=ALU.mult,
            )

        def scale_and_shift(unit):
            node_tile = unit // GROUPS
            for gi, g in enumerate(graphs_of(unit)):
                nc.vector.tensor_scalar(
                    out=result[unit][:, gi, :],
                    in0=result[unit][:, gi, :],
                    scalar1=factor[node_tile][:, g : g + 1],
                    scalar2=shift[node_tile][:, 0:1],
                    op0=ALU.mult,
                    op1=ALU.add,
                )

        def store(unit):
            first = graphs_of(unit)[0]
            nc.sync.dma_start(out=out_rows[:, first : first + PAIR, unit // GROUPS, :], in_=result[unit][:])

        def run(stage, unit):
            if 0 <= unit < UNITS:
                stage(unit)

        for step in range(UNITS + LAG_STORE):
            run(store, step - LAG_STORE)
            run(scale_and_shift, step - LAG_APPLY)
            run(factors, step - LAG_FACTORS)
            run(moments, step - LAG_MOMENTS)
            run(norms, step - LAG_NORMS)
            run(relu_statistics, step - LAG_STATS)
            run(relu_and_square_sum, step - LAG_RELU)
            run(add_bias, step - LAG_BIAS)
            run(multiply_h, step - LAG_H)
            run(quantise_agg, step - LAG_AGG_QUANT)
            run(copy_agg_out, step - LAG_AGG_OUT)
            run(multiply_agg, step - LAG_AGG)
            run(quantise_adj, step - LAG_ADJ_QUANT)
            run(copy_adj_out, step - LAG_ADJ_OUT)
            run(transpose_adj, step - LAG_TRANSPOSE)
            run(quantise_x, step - LAG_X_QUANT)
            run(regroup_x, step - LAG_X_REGROUP)
            run(load, step - LAG_LOAD)
            if step == 0:
                prepare_constants()
